import numpy as np
import ml_dtypes

BF16 = ml_dtypes.bfloat16


def bf(x):
    return np.asarray(x, np.float32).astype(BF16)


def f32(x):
    return np.asarray(x, np.float32)


def f64(x):
    return np.asarray(x).astype(np.float64)


def striped(idx):
    return np.tile(idx.reshape(-1, 16).T, (8, 1))


C, S, D, N, H, R, HOPS = 128, 256, 4, 1024, 128, 8, 2
TWO_SIGMA_SQ = 2.0 * (0.1 * 0.1)
EPS = 0.005


def setup_inputs():
    mu = np.random.standard_normal((C, 1))
    amp = np.random.uniform(0.4, 1.6, (1, S))
    x = f32(mu + EPS * amp * np.random.standard_normal((C, S)))
    weight = f32(np.random.uniform(0.3, 0.7, (1, HOPS + 1)))
    idx = np.concatenate([np.random.permutation(S)[:H] for _ in range(R)])
    return {"x": x, "weight": weight, "offs": striped(idx)}


def reference(x, weight, offs):
    idx = offs[:16].T.reshape(-1)
    xx = f64(x)
    w = f64(weight)
    diff = xx[:, idx] + (-np.tile(xx, (1, D)))
    sq = (diff ** 2).reshape(C, D, S).sum(axis=(0, 1))
    kern = np.exp(-sq / TWO_SIGMA_SQ)
    return w[0, 0] * np.maximum(xx, 0.0) + w[0, 1:].sum() * kern[None, :]

@@ -1,0 +1,63 @@
+import concourse.mybir as mybir
+
+F32, BF16, U16 = mybir.dt.float32, mybir.dt.bfloat16, mybir.dt.uint16
+ADD, MULT, MAX = mybir.AluOpType.add, mybir.AluOpType.mult, mybir.AluOpType.max
+SQUARE, EXP = mybir.ActivationFunctionType.Square, mybir.ActivationFunctionType.Exp
+
+C = 128
+S = 256
+D = 4
+N = D * S
+TWO_SIGMA_SQ = 0.02
+PER_COLUMN = 16
+
+FLOPS = 3 * C * N + 4 * C * S
+
+
+def tile_kernelgaactivation_kernel(tc, x, weight, offs, out):
+    nc = tc.nc
+    with (
+        tc.tile_pool(name="held", bufs=1) as held,
+        tc.tile_pool(name="ring", bufs=D) as ring,
+        tc.psum_pool(name="psum", bufs=1) as psum,
+    ):
+        offsets = held.tile([C, N // PER_COLUMN], U16, name="offsets")
+        nc.sync.dma_start(offsets[:], offs)
+        nodes = held.tile([C, S], F32, name="nodes")
+        nc.scalar.dma_start(nodes[:], x)
+        mix = held.tile([C, 3], F32, name="mix")
+        nc.gpsimd.dma_start(mix[:], weight.rearrange("a b -> (a b)").partition_broadcast(C))
+
+        negated = held.tile([C, S], F32, name="negated")
+        nc.vector.tensor_scalar_mul(negated[:], nodes[:], -1.0)
+
+        ones = held.tile([C, C], BF16, name="ones")
+        nc.gpsimd.memset(ones[:], 1.0)
+
+        total = None
+        for d in range(D):
+            piece = offsets[:, d * (S // PER_COLUMN) : (d + 1) * (S // PER_COLUMN)]
+            diff = ring.tile([C, S], F32, name="diff")
+            nc.vector.tensor_tensor(diff[:], nodes[:].indirect(piece), negated[:], ADD)
+            square = ring.tile([C, S], F32, name="square")
+            nc.scalar.activation(square[:], diff[:], SQUARE)
+            if d == 0:
+                total = square
+            else:
+                summed = ring.tile([C, S], BF16 if d == D - 1 else F32, name=f"summed{d}")
+                nc.vector.tensor_tensor(summed[:], total[:], square[:], ADD)
+                total = summed
+
+        sq = psum.tile([C, S], F32, name="sq")
+        nc.tensor.matmul(sq[:], ones[:], total[:], start=True, stop=True)
+        kern = held.tile([C, S], F32, name="kern")
+        nc.scalar.activation(kern[:], sq[:], EXP, scale=-1.0 / TWO_SIGMA_SQ)
+
+        own = held.tile([C, S], F32, name="own")
+        nc.vector.tensor_scalar(own[:], nodes[:], 0.0, mix[:, 0:1], op0=MAX, op1=MULT)
+        kern_weight = held.tile([C, 1], F32, name="kern_weight")
+        nc.vector.tensor_tensor(kern_weight[:], mix[:, 1:2], mix[:, 2:3], ADD)
+
+        result = held.tile([C, S], F32, name="result")
+        nc.vector.scalar_tensor_tensor(result[:], kern[:], kern_weight[:], own[:], op0=MULT, op1=ADD)
+        nc.sync.dma_start(out, result[:])

@@ -26,7 +26,7 @@ def tile_kernelgaactivation_kernel(tc, x, weight, offs, out):
         nodes = held.tile([C, S], F32, name="nodes")
         nc.scalar.dma_start(nodes[:], x)
         mix = held.tile([C, 3], F32, name="mix")
-        nc.gpsimd.dma_start(mix[:], weight.rearrange("a b -> (a b)").partition_broadcast(C))
+        nc.sync.dma_start(mix[:], weight.rearrange("a b -> (a b)").partition_broadcast(C))
 
         negated = held.tile([C, S], F32, name="negated")
         nc.vector.tensor_scalar_mul(negated[:], nodes[:], -1.0)
@@ -44,8 +44,10 @@ def tile_kernelgaactivation_kernel(tc, x, weight, offs, out):
             if d == 0:
                 total = square
             else:
-                summed = ring.tile([C, S], BF16 if d == D - 1 else F32, name=f"summed{d}")
-                nc.vector.tensor_tensor(summed[:], total[:], square[:], ADD)
+                last = d == D - 1
+                summed = ring.tile([C, S], BF16 if last else F32, name=f"summed{d}")
+                adder = nc.vector if last else nc.gpsimd
+                adder.tensor_tensor(summed[:], total[:], square[:], ADD)
                 total = summed
 
         sq = psum.tile([C, S], F32, name="sq")
@@ -56,7 +58,7 @@ def tile_kernelgaactivation_kernel(tc, x, weight, offs, out):
         own = held.tile([C, S], F32, name="own")
         nc.vector.tensor_scalar(own[:], nodes[:], 0.0, mix[:, 0:1], op0=MAX, op1=MULT)
         kern_weight = held.tile([C, 1], F32, name="kern_weight")
-        nc.vector.tensor_tensor(kern_weight[:], mix[:, 1:2], mix[:, 2:3], ADD)
+        nc.gpsimd.tensor_tensor(kern_weight[:], mix[:, 1:2], mix[:, 2:3], ADD)
 
         result = held.tile([C, S], F32, name="result")
         nc.vector.scalar_tensor_tensor(result[:], kern[:], kern_weight[:], own[:], op0=MULT, op1=ADD)

@@ -34,6 +34,7 @@ def tile_kernelgaactivation_kernel(tc, x, weight, offs, out):
         ones = held.tile([C, C], BF16, name="ones")
         nc.gpsimd.memset(ones[:], 1.0)
 
+        squares = []
         total = None
         for d in range(D):
             piece = offsets[:, d * (S // PER_COLUMN) : (d + 1) * (S // PER_COLUMN)]
@@ -41,17 +42,18 @@ def tile_kernelgaactivation_kernel(tc, x, weight, offs, out):
             nc.vector.tensor_tensor(diff[:], nodes[:].indirect(piece), negated[:], ADD)
             square = ring.tile([C, S], F32, name="square")
             nc.scalar.activation(square[:], diff[:], SQUARE)
+            squares.append(square)
             if d == 0:
                 total = square
-            else:
-                last = d == D - 1
-                summed = ring.tile([C, S], BF16 if last else F32, name=f"summed{d}")
-                adder = nc.vector if last else nc.gpsimd
-                adder.tensor_tensor(summed[:], total[:], square[:], ADD)
+            if d >= 2:
+                summed = ring.tile([C, S], F32, name="summed")
+                nc.vector.tensor_tensor(summed[:], total[:], squares[d - 1][:], ADD)
                 total = summed
+        q = held.tile([C, S], BF16, name="q")
+        nc.vector.tensor_tensor(q[:], total[:], squares[D - 1][:], ADD)
 
         sq = psum.tile([C, S], F32, name="sq")
-        nc.tensor.matmul(sq[:], ones[:], total[:], start=True, stop=True)
+        nc.tensor.matmul(sq[:], ones[:], q[:], start=True, stop=True)
         kern = held.tile([C, S], F32, name="kern")
         nc.scalar.activation(kern[:], sq[:], EXP, scale=-1.0 / TWO_SIGMA_SQ)
 

@@ -10,6 +10,7 @@ D = 4
 N = D * S
 TWO_SIGMA_SQ = 0.02
 PER_COLUMN = 16
+TAIL_BLOCKS = 2
 
 FLOPS = 3 * C * N + 4 * C * S
 
@@ -18,7 +19,6 @@ def tile_kernelgaactivation_kernel(tc, x, weight, offs, out):
     nc = tc.nc
     with (
         tc.tile_pool(name="held", bufs=1) as held,
-        tc.tile_pool(name="ring", bufs=D) as ring,
         tc.psum_pool(name="psum", bufs=1) as psum,
     ):
         offsets = held.tile([C, N // PER_COLUMN], U16, name="offsets")
@@ -34,34 +34,51 @@ def tile_kernelgaactivation_kernel(tc, x, weight, offs, out):
         ones = held.tile([C, C], BF16, name="ones")
         nc.gpsimd.memset(ones[:], 1.0)
 
+        block = S // TAIL_BLOCKS
+        blocks = [(b * block, (b + 1) * block) for b in range(TAIL_BLOCKS)]
+        pieces = [(d, 0, S) for d in range(D - 1)] + [(D - 1, lo, hi) for lo, hi in blocks]
+
+        q = held.tile([C, S], BF16, name="q")
         squares = []
-        total = None
-        for d in range(D):
-            piece = offsets[:, d * (S // PER_COLUMN) : (d + 1) * (S // PER_COLUMN)]
-            diff = ring.tile([C, S], F32, name="diff")
-            nc.vector.tensor_tensor(diff[:], nodes[:].indirect(piece), negated[:], ADD)
-            square = ring.tile([C, S], F32, name="square")
+        totals = []
+
+        def add_square(i):
+            d, lo, hi = pieces[i]
+            if d < D - 1:
+                summed = held.tile([C, S], F32, name=f"summed{i}")
+                nc.vector.tensor_tensor(summed[:], totals[-1][:], squares[i][:], ADD)
+                totals.append(summed)
+            else:
+                nc.vector.tensor_tensor(q[:, lo:hi], totals[-1][:, lo:hi], squares[i][:], ADD)
+
+        for i, (d, lo, hi) in enumerate(pieces):
+            first = (d * S + lo) // PER_COLUMN
+            piece = offsets[:, first : first + (hi - lo) // PER_COLUMN]
+            diff = held.tile([C, hi - lo], F32, name=f"diff{i}")
+            nc.vector.tensor_tensor(diff[:], nodes[:].indirect(piece), negated[:, lo:hi], ADD)
+            square = held.tile([C, hi - lo], F32, name=f"square{i}")
             nc.scalar.activation(square[:], diff[:], SQUARE)
             squares.append(square)
-            if d == 0:
-                total = square
-            if d >= 2:
-                summed = ring.tile([C, S], F32, name="summed")
-                nc.vector.tensor_tensor(summed[:], total[:], squares[d - 1][:], ADD)
-                total = summed
-        q = held.tile([C, S], BF16, name="q")
-        nc.vector.tensor_tensor(q[:], total[:], squares[D - 1][:], ADD)
-
-        sq = psum.tile([C, S], F32, name="sq")
-        nc.tensor.matmul(sq[:], ones[:], q[:], start=True, stop=True)
-        kern = held.tile([C, S], F32, name="kern")
-        nc.scalar.activation(kern[:], sq[:], EXP, scale=-1.0 / TWO_SIGMA_SQ)
+            if i == 0:
+                totals.append(square)
+            if i >= 2:
+                add_square(i - 1)
+        add_square(len(pieces) - 1)
 
         own = held.tile([C, S], F32, name="own")
         nc.vector.tensor_scalar(own[:], nodes[:], 0.0, mix[:, 0:1], op0=MAX, op1=MULT)
         kern_weight = held.tile([C, 1], F32, name="kern_weight")
         nc.gpsimd.tensor_tensor(kern_weight[:], mix[:, 1:2], mix[:, 2:3], ADD)
 
+        sums = [psum.tile([C, block], F32, name=f"sq{b}") for b in range(TAIL_BLOCKS)]
+        for sq, (lo, hi) in zip(sums, blocks):
+            nc.tensor.matmul(sq[:], ones[:], q[:, lo:hi], start=True, stop=True)
+        kern = held.tile([C, S], F32, name="kern")
+        for sq, (lo, hi) in zip(sums, blocks):
+            nc.scalar.activation(kern[:, lo:hi], sq[:], EXP, scale=-1.0 / TWO_SIGMA_SQ)
         result = held.tile([C, S], F32, name="result")
-        nc.vector.scalar_tensor_tensor(result[:], kern[:], kern_weight[:], own[:], op0=MULT, op1=ADD)
-        nc.sync.dma_start(out, result[:])
+        for lo, hi in blocks:
+            nc.vector.scalar_tensor_tensor(
+                result[:, lo:hi], kern[:, lo:hi], kern_weight[:], own[:, lo:hi], op0=MULT, op1=ADD
+            )
+            nc.sync.dma_start(out[:, lo:hi], result[:, lo:hi])

@@ -10,7 +10,7 @@ D = 4
 N = D * S
 TWO_SIGMA_SQ = 0.02
 PER_COLUMN = 16
-TAIL_BLOCKS = 2
+HALF = S // 2
 
 FLOPS = 3 * C * N + 4 * C * S
 
@@ -34,50 +34,40 @@ def tile_kernelgaactivation_kernel(tc, x, weight, offs, out):
         ones = held.tile([C, C], BF16, name="ones")
         nc.gpsimd.memset(ones[:], 1.0)
 
-        block = S // TAIL_BLOCKS
-        blocks = [(b * block, (b + 1) * block) for b in range(TAIL_BLOCKS)]
-        pieces = [(d, 0, S) for d in range(D - 1)] + [(D - 1, lo, hi) for lo, hi in blocks]
-
-        q = held.tile([C, S], BF16, name="q")
         squares = []
-        totals = []
-
-        def add_square(i):
-            d, lo, hi = pieces[i]
-            if d < D - 1:
-                summed = held.tile([C, S], F32, name=f"summed{i}")
-                nc.vector.tensor_tensor(summed[:], totals[-1][:], squares[i][:], ADD)
-                totals.append(summed)
-            else:
-                nc.vector.tensor_tensor(q[:, lo:hi], totals[-1][:, lo:hi], squares[i][:], ADD)
-
-        for i, (d, lo, hi) in enumerate(pieces):
-            first = (d * S + lo) // PER_COLUMN
-            piece = offsets[:, first : first + (hi - lo) // PER_COLUMN]
-            diff = held.tile([C, hi - lo], F32, name=f"diff{i}")
-            nc.vector.tensor_tensor(diff[:], nodes[:].indirect(piece), negated[:, lo:hi], ADD)
-            square = held.tile([C, hi - lo], F32, name=f"square{i}")
+        for d in range(D):
+            piece = offsets[:, d * (S // PER_COLUMN) : (d + 1) * (S // PER_COLUMN)]
+            diff = held.tile([C, S], F32, name=f"diff{d}")
+            nc.vector.tensor_tensor(diff[:], nodes[:].indirect(piece), negated[:], ADD)
+            square = held.tile([C, S], F32, name=f"square{d}")
             nc.scalar.activation(square[:], diff[:], SQUARE)
             squares.append(square)
-            if i == 0:
-                totals.append(square)
-            if i >= 2:
-                add_square(i - 1)
-        add_square(len(pieces) - 1)
+
+        total = squares[0]
+        for d in range(1, D - 1):
+            summed = held.tile([C, S], F32, name=f"summed{d}")
+            nc.vector.tensor_tensor(summed[:], total[:], squares[d][:], ADD)
+            total = summed
+
+        halves = [(0, HALF), (HALF, S)]
+
+        q = held.tile([C, S], BF16, name="q")
+        for lo, hi in halves:
+            nc.vector.tensor_tensor(q[:, lo:hi], total[:, lo:hi], squares[D - 1][:, lo:hi], ADD)
 
         own = held.tile([C, S], F32, name="own")
         nc.vector.tensor_scalar(own[:], nodes[:], 0.0, mix[:, 0:1], op0=MAX, op1=MULT)
         kern_weight = held.tile([C, 1], F32, name="kern_weight")
         nc.gpsimd.tensor_tensor(kern_weight[:], mix[:, 1:2], mix[:, 2:3], ADD)
 
-        sums = [psum.tile([C, block], F32, name=f"sq{b}") for b in range(TAIL_BLOCKS)]
-        for sq, (lo, hi) in zip(sums, blocks):
+        sums = [psum.tile([C, HALF], F32, name=f"sq{lo}") for lo, hi in halves]
+        for sq, (lo, hi) in zip(sums, halves):
             nc.tensor.matmul(sq[:], ones[:], q[:, lo:hi], start=True, stop=True)
         kern = held.tile([C, S], F32, name="kern")
-        for sq, (lo, hi) in zip(sums, blocks):
+        for sq, (lo, hi) in zip(sums, halves):
             nc.scalar.activation(kern[:, lo:hi], sq[:], EXP, scale=-1.0 / TWO_SIGMA_SQ)
         result = held.tile([C, S], F32, name="result")
-        for lo, hi in blocks:
+        for lo, hi in halves:
             nc.vector.scalar_tensor_tensor(
                 result[:, lo:hi], kern[:, lo:hi], kern_weight[:], own[:, lo:hi], op0=MULT, op1=ADD
             )

@@ -46,7 +46,8 @@ def tile_kernelgaactivation_kernel(tc, x, weight, offs, out):
         total = squares[0]
         for d in range(1, D - 1):
             summed = held.tile([C, S], F32, name=f"summed{d}")
-            nc.vector.tensor_tensor(summed[:], total[:], squares[d][:], ADD)
+            adder = nc.gpsimd if d == 1 else nc.vector
+            adder.tensor_tensor(summed[:], total[:], squares[d][:], ADD)
             total = summed
 
         halves = [(0, HALF), (HALF, S)]

@@ -1,8 +1,10 @@
 import concourse.mybir as mybir
 
 F32, BF16, U16 = mybir.dt.float32, mybir.dt.bfloat16, mybir.dt.uint16
-ADD, MULT, MAX = mybir.AluOpType.add, mybir.AluOpType.mult, mybir.AluOpType.max
+ADD, MULT = mybir.AluOpType.add, mybir.AluOpType.mult
 SQUARE, EXP = mybir.ActivationFunctionType.Square, mybir.ActivationFunctionType.Exp
+RELU, COPY = mybir.ActivationFunctionType.Relu, mybir.ActivationFunctionType.Copy
+IDENTITY = mybir.ActivationFunctionType.Identity
 
 C = 128
 S = 256
@@ -34,6 +36,13 @@ def tile_kernelgaactivation_kernel(tc, x, weight, offs, out):
         ones = held.tile([C, C], BF16, name="ones")
         nc.gpsimd.memset(ones[:], 1.0)
 
+        relu = held.tile([C, S], F32, name="relu")
+        nc.scalar.activation(relu[:], nodes[:], RELU)
+        own = held.tile([C, S], F32, name="own")
+        nc.scalar.activation(own[:], relu[:], COPY, scale=mix[:, 0:1])
+        kern_weight = held.tile([C, 1], F32, name="kern_weight")
+        nc.scalar.activation(kern_weight[:], mix[:, 1:2], IDENTITY, bias=mix[:, 2:3])
+
         squares = []
         for d in range(D):
             piece = offsets[:, d * (S // PER_COLUMN) : (d + 1) * (S // PER_COLUMN)]
@@ -46,8 +55,7 @@ def tile_kernelgaactivation_kernel(tc, x, weight, offs, out):
         total = squares[0]
         for d in range(1, D - 1):
             summed = held.tile([C, S], F32, name=f"summed{d}")
-            adder = nc.gpsimd if d == 1 else nc.vector
-            adder.tensor_tensor(summed[:], total[:], squares[d][:], ADD)
+            nc.vector.tensor_tensor(summed[:], total[:], squares[d][:], ADD)
             total = summed
 
         halves = [(0, HALF), (HALF, S)]
@@ -55,11 +63,6 @@ def tile_kernelgaactivation_kernel(tc, x, weight, offs, out):
         q = held.tile([C, S], BF16, name="q")
         for lo, hi in halves:
             nc.vector.tensor_tensor(q[:, lo:hi], total[:, lo:hi], squares[D - 1][:, lo:hi], ADD)
-
-        own = held.tile([C, S], F32, name="own")
-        nc.vector.tensor_scalar(own[:], nodes[:], 0.0, mix[:, 0:1], op0=MAX, op1=MULT)
-        kern_weight = held.tile([C, 1], F32, name="kern_weight")
-        nc.gpsimd.tensor_tensor(kern_weight[:], mix[:, 1:2], mix[:, 2:3], ADD)
 
         sums = [psum.tile([C, HALF], F32, name=f"sq{lo}") for lo, hi in halves]
         for sq, (lo, hi) in zip(sums, halves):

@@ -43,30 +43,18 @@ def tile_kernelgaactivation_kernel(tc, x, weight, offs, out):
         kern_weight = held.tile([C, 1], F32, name="kern_weight")
         nc.scalar.activation(kern_weight[:], mix[:, 1:2], IDENTITY, bias=mix[:, 2:3])
 
-        squares = []
+        halves = [(0, HALF), (HALF, S)]
+        sums = [psum.tile([C, HALF], F32, name=f"sq{lo}") for lo, hi in halves]
+
         for d in range(D):
             piece = offsets[:, d * (S // PER_COLUMN) : (d + 1) * (S // PER_COLUMN)]
             diff = held.tile([C, S], F32, name=f"diff{d}")
             nc.vector.tensor_tensor(diff[:], nodes[:].indirect(piece), negated[:], ADD)
-            square = held.tile([C, S], F32, name=f"square{d}")
+            square = held.tile([C, S], BF16, name=f"square{d}")
             nc.scalar.activation(square[:], diff[:], SQUARE)
-            squares.append(square)
+            for sq, (lo, hi) in zip(sums, halves):
+                nc.tensor.matmul(sq[:], ones[:], square[:, lo:hi], start=(d == 0), stop=(d == D - 1))
 
-        total = squares[0]
-        for d in range(1, D - 1):
-            summed = held.tile([C, S], F32, name=f"summed{d}")
-            nc.vector.tensor_tensor(summed[:], total[:], squares[d][:], ADD)
-            total = summed
-
-        halves = [(0, HALF), (HALF, S)]
-
-        q = held.tile([C, S], BF16, name="q")
-        for lo, hi in halves:
-            nc.vector.tensor_tensor(q[:, lo:hi], total[:, lo:hi], squares[D - 1][:, lo:hi], ADD)
-
-        sums = [psum.tile([C, HALF], F32, name=f"sq{lo}") for lo, hi in halves]
-        for sq, (lo, hi) in zip(sums, halves):
-            nc.tensor.matmul(sq[:], ones[:], q[:, lo:hi], start=True, stop=True)
         kern = held.tile([C, S], F32, name="kern")
         for sq, (lo, hi) in zip(sums, halves):
             nc.scalar.activation(kern[:, lo:hi], sq[:], EXP, scale=-1.0 / TWO_SIGMA_SQ)

@@ -12,7 +12,8 @@ D = 4
 N = D * S
 TWO_SIGMA_SQ = 0.02
 PER_COLUMN = 16
-HALF = S // 2
+BLOCKS = [(0, 128), (128, 256)]
+EXP_LAG = 2
 
 FLOPS = 3 * C * N + 4 * C * S
 
@@ -43,23 +44,27 @@ def tile_kernelgaactivation_kernel(tc, x, weight, offs, out):
         kern_weight = held.tile([C, 1], F32, name="kern_weight")
         nc.scalar.activation(kern_weight[:], mix[:, 1:2], IDENTITY, bias=mix[:, 2:3])
 
-        halves = [(0, HALF), (HALF, S)]
-        sums = [psum.tile([C, HALF], F32, name=f"sq{lo}") for lo, hi in halves]
-
-        for d in range(D):
-            piece = offsets[:, d * (S // PER_COLUMN) : (d + 1) * (S // PER_COLUMN)]
-            diff = held.tile([C, S], F32, name=f"diff{d}")
-            nc.vector.tensor_tensor(diff[:], nodes[:].indirect(piece), negated[:], ADD)
-            square = held.tile([C, S], BF16, name=f"square{d}")
-            nc.scalar.activation(square[:], diff[:], SQUARE)
-            for sq, (lo, hi) in zip(sums, halves):
-                nc.tensor.matmul(sq[:], ones[:], square[:, lo:hi], start=(d == 0), stop=(d == D - 1))
-
+        sums = [psum.tile([C, hi - lo], F32, name=f"sq{lo}") for lo, hi in BLOCKS]
         kern = held.tile([C, S], F32, name="kern")
-        for sq, (lo, hi) in zip(sums, halves):
-            nc.scalar.activation(kern[:, lo:hi], sq[:], EXP, scale=-1.0 / TWO_SIGMA_SQ)
+
+        def gaussian(b):
+            lo, hi = BLOCKS[b]
+            nc.scalar.activation(kern[:, lo:hi], sums[b][:], EXP, scale=-1.0 / TWO_SIGMA_SQ)
+
+        for b, (lo, hi) in enumerate(BLOCKS):
+            for d in range(D):
+                piece = offsets[:, (d * S + lo) // PER_COLUMN : (d * S + hi) // PER_COLUMN]
+                diff = held.tile([C, hi - lo], F32, name=f"diff{b}_{d}")
+                nc.vector.tensor_tensor(diff[:], nodes[:].indirect(piece), negated[:, lo:hi], ADD)
+                square = held.tile([C, hi - lo], BF16, name=f"square{b}_{d}")
+                nc.scalar.activation(square[:], diff[:], SQUARE)
+                nc.tensor.matmul(sums[b][:], ones[:], square[:], start=(d == 0), stop=(d == D - 1))
+                if b > 0 and d == EXP_LAG - 1:
+                    gaussian(b - 1)
+        gaussian(len(BLOCKS) - 1)
+
         result = held.tile([C, S], F32, name="result")
-        for lo, hi in halves:
+        for lo, hi in BLOCKS:
             nc.vector.scalar_tensor_tensor(
                 result[:, lo:hi], kern[:, lo:hi], kern_weight[:], own[:, lo:hi], op0=MULT, op1=ADD
             )

@@ -1,9 +1,8 @@
 import concourse.mybir as mybir
 
 F32, BF16, U16 = mybir.dt.float32, mybir.dt.bfloat16, mybir.dt.uint16
-ADD, MULT = mybir.AluOpType.add, mybir.AluOpType.mult
+ADD, MULT, MAX = mybir.AluOpType.add, mybir.AluOpType.mult, mybir.AluOpType.max
 SQUARE, EXP = mybir.ActivationFunctionType.Square, mybir.ActivationFunctionType.Exp
-RELU, COPY = mybir.ActivationFunctionType.Relu, mybir.ActivationFunctionType.Copy
 IDENTITY = mybir.ActivationFunctionType.Identity
 
 C = 128
@@ -37,10 +36,6 @@ def tile_kernelgaactivation_kernel(tc, x, weight, offs, out):
         ones = held.tile([C, C], BF16, name="ones")
         nc.gpsimd.memset(ones[:], 1.0)
 
-        relu = held.tile([C, S], F32, name="relu")
-        nc.scalar.activation(relu[:], nodes[:], RELU)
-        own = held.tile([C, S], F32, name="own")
-        nc.scalar.activation(own[:], relu[:], COPY, scale=mix[:, 0:1])
         kern_weight = held.tile([C, 1], F32, name="kern_weight")
         nc.scalar.activation(kern_weight[:], mix[:, 1:2], IDENTITY, bias=mix[:, 2:3])
 
@@ -63,8 +58,10 @@ def tile_kernelgaactivation_kernel(tc, x, weight, offs, out):
                     gaussian(b - 1)
         gaussian(len(BLOCKS) - 1)
 
+        own = held.tile([C, S], F32, name="own")
         result = held.tile([C, S], F32, name="result")
         for lo, hi in BLOCKS:
+            nc.vector.tensor_scalar(own[:, lo:hi], nodes[:, lo:hi], 0.0, mix[:, 0:1], op0=MAX, op1=MULT)
             nc.vector.scalar_tensor_tensor(
                 result[:, lo:hi], kern[:, lo:hi], kern_weight[:], own[:, lo:hi], op0=MULT, op1=ADD
             )

@@ -11,8 +11,7 @@ D = 4
 N = D * S
 TWO_SIGMA_SQ = 0.02
 PER_COLUMN = 16
-BLOCKS = [(0, 128), (128, 256)]
-EXP_LAG = 2
+HALVES = [(0, 128), (128, 256)]
 
 FLOPS = 3 * C * N + 4 * C * S
 
@@ -39,29 +38,29 @@ def tile_kernelgaactivation_kernel(tc, x, weight, offs, out):
         kern_weight = held.tile([C, 1], F32, name="kern_weight")
         nc.scalar.activation(kern_weight[:], mix[:, 1:2], IDENTITY, bias=mix[:, 2:3])
 
-        sums = [psum.tile([C, hi - lo], F32, name=f"sq{lo}") for lo, hi in BLOCKS]
-        kern = held.tile([C, S], F32, name="kern")
+        sums = [psum.tile([C, hi - lo], F32, name=f"sq{lo}") for lo, hi in HALVES]
 
-        def gaussian(b):
-            lo, hi = BLOCKS[b]
-            nc.scalar.activation(kern[:, lo:hi], sums[b][:], EXP, scale=-1.0 / TWO_SIGMA_SQ)
-
-        for b, (lo, hi) in enumerate(BLOCKS):
-            for d in range(D):
+        for d in range(D):
+            for lo, hi in HALVES if d == D - 1 else [(0, S)]:
                 piece = offsets[:, (d * S + lo) // PER_COLUMN : (d * S + hi) // PER_COLUMN]
-                diff = held.tile([C, hi - lo], F32, name=f"diff{b}_{d}")
+                diff = held.tile([C, hi - lo], F32, name=f"diff{d}_{lo}")
                 nc.vector.tensor_tensor(diff[:], nodes[:].indirect(piece), negated[:, lo:hi], ADD)
-                square = held.tile([C, hi - lo], BF16, name=f"square{b}_{d}")
+                square = held.tile([C, hi - lo], BF16, name=f"square{d}_{lo}")
                 nc.scalar.activation(square[:], diff[:], SQUARE)
-                nc.tensor.matmul(sums[b][:], ones[:], square[:], start=(d == 0), stop=(d == D - 1))
-                if b > 0 and d == EXP_LAG - 1:
-                    gaussian(b - 1)
-        gaussian(len(BLOCKS) - 1)
+                for sq, (half_lo, half_hi) in zip(sums, HALVES):
+                    if lo <= half_lo and half_hi <= hi:
+                        nc.tensor.matmul(
+                            sq[:], ones[:], square[:, half_lo - lo : half_hi - lo], start=(d == 0), stop=(d == D - 1)
+                        )
+
+        kern = held.tile([C, S], F32, name="kern")
+        for sq, (lo, hi) in zip(sums, HALVES):
+            nc.scalar.activation(kern[:, lo:hi], sq[:], EXP, scale=-1.0 / TWO_SIGMA_SQ)
 
         own = held.tile([C, S], F32, name="own")
+        nc.vector.tensor_scalar(own[:], nodes[:], 0.0, mix[:, 0:1], op0=MAX, op1=MULT)
         result = held.tile([C, S], F32, name="result")
-        for lo, hi in BLOCKS:
-            nc.vector.tensor_scalar(own[:, lo:hi], nodes[:, lo:hi], 0.0, mix[:, 0:1], op0=MAX, op1=MULT)
+        for lo, hi in HALVES:
             nc.vector.scalar_tensor_tensor(
                 result[:, lo:hi], kern[:, lo:hi], kern_weight[:], own[:, lo:hi], op0=MULT, op1=ADD
             )

@@ -11,7 +11,7 @@ D = 4
 N = D * S
 TWO_SIGMA_SQ = 0.02
 PER_COLUMN = 16
-HALVES = [(0, 128), (128, 256)]
+PARTS = [(0, 128), (128, 192), (192, 256)]
 
 FLOPS = 3 * C * N + 4 * C * S
 
@@ -38,29 +38,29 @@ def tile_kernelgaactivation_kernel(tc, x, weight, offs, out):
         kern_weight = held.tile([C, 1], F32, name="kern_weight")
         nc.scalar.activation(kern_weight[:], mix[:, 1:2], IDENTITY, bias=mix[:, 2:3])
 
-        sums = [psum.tile([C, hi - lo], F32, name=f"sq{lo}") for lo, hi in HALVES]
+        sums = [psum.tile([C, hi - lo], F32, name=f"sq{lo}") for lo, hi in PARTS]
 
         for d in range(D):
-            for lo, hi in HALVES if d == D - 1 else [(0, S)]:
+            for lo, hi in PARTS if d == D - 1 else [(0, S)]:
                 piece = offsets[:, (d * S + lo) // PER_COLUMN : (d * S + hi) // PER_COLUMN]
                 diff = held.tile([C, hi - lo], F32, name=f"diff{d}_{lo}")
                 nc.vector.tensor_tensor(diff[:], nodes[:].indirect(piece), negated[:, lo:hi], ADD)
                 square = held.tile([C, hi - lo], BF16, name=f"square{d}_{lo}")
                 nc.scalar.activation(square[:], diff[:], SQUARE)
-                for sq, (half_lo, half_hi) in zip(sums, HALVES):
-                    if lo <= half_lo and half_hi <= hi:
+                for sq, (part_lo, part_hi) in zip(sums, PARTS):
+                    if lo <= part_lo and part_hi <= hi:
                         nc.tensor.matmul(
-                            sq[:], ones[:], square[:, half_lo - lo : half_hi - lo], start=(d == 0), stop=(d == D - 1)
+                            sq[:], ones[:], square[:, part_lo - lo : part_hi - lo], start=(d == 0), stop=(d == D - 1)
                         )
 
         kern = held.tile([C, S], F32, name="kern")
-        for sq, (lo, hi) in zip(sums, HALVES):
+        for sq, (lo, hi) in zip(sums, PARTS):
             nc.scalar.activation(kern[:, lo:hi], sq[:], EXP, scale=-1.0 / TWO_SIGMA_SQ)
 
         own = held.tile([C, S], F32, name="own")
         nc.vector.tensor_scalar(own[:], nodes[:], 0.0, mix[:, 0:1], op0=MAX, op1=MULT)
         result = held.tile([C, S], F32, name="result")
-        for lo, hi in HALVES:
+        for lo, hi in PARTS:
             nc.vector.scalar_tensor_tensor(
                 result[:, lo:hi], kern[:, lo:hi], kern_weight[:], own[:, lo:hi], op0=MULT, op1=ADD
             )

@@ -11,7 +11,13 @@ D = 4
 N = D * S
 TWO_SIGMA_SQ = 0.02
 PER_COLUMN = 16
+HALVES = [(0, 128), (128, 256)]
 PARTS = [(0, 128), (128, 192), (192, 256)]
+LOOK_UPS = (
+    [(0, (0, S)), (1, (0, S))]
+    + [(2, HALVES[0]), (3, HALVES[0])]
+    + [(2, HALVES[1]), (3, PARTS[1]), (3, PARTS[2])]
+)
 
 FLOPS = 3 * C * N + 4 * C * S
 
@@ -40,18 +46,17 @@ def tile_kernelgaactivation_kernel(tc, x, weight, offs, out):
 
         sums = [psum.tile([C, hi - lo], F32, name=f"sq{lo}") for lo, hi in PARTS]
 
-        for d in range(D):
-            for lo, hi in PARTS if d == D - 1 else [(0, S)]:
-                piece = offsets[:, (d * S + lo) // PER_COLUMN : (d * S + hi) // PER_COLUMN]
-                diff = held.tile([C, hi - lo], F32, name=f"diff{d}_{lo}")
-                nc.vector.tensor_tensor(diff[:], nodes[:].indirect(piece), negated[:, lo:hi], ADD)
-                square = held.tile([C, hi - lo], BF16, name=f"square{d}_{lo}")
-                nc.scalar.activation(square[:], diff[:], SQUARE)
-                for sq, (part_lo, part_hi) in zip(sums, PARTS):
-                    if lo <= part_lo and part_hi <= hi:
-                        nc.tensor.matmul(
-                            sq[:], ones[:], square[:, part_lo - lo : part_hi - lo], start=(d == 0), stop=(d == D - 1)
-                        )
+        for d, (lo, hi) in LOOK_UPS:
+            piece = offsets[:, (d * S + lo) // PER_COLUMN : (d * S + hi) // PER_COLUMN]
+            diff = held.tile([C, hi - lo], F32, name=f"diff{d}_{lo}")
+            nc.vector.tensor_tensor(diff[:], nodes[:].indirect(piece), negated[:, lo:hi], ADD)
+            square = held.tile([C, hi - lo], BF16, name=f"square{d}_{lo}")
+            nc.scalar.activation(square[:], diff[:], SQUARE)
+            for sq, (part_lo, part_hi) in zip(sums, PARTS):
+                if lo <= part_lo and part_hi <= hi:
+                    nc.tensor.matmul(
+                        sq[:], ones[:], square[:, part_lo - lo : part_hi - lo], start=(d == 0), stop=(d == D - 1)
+                    )
 
         kern = held.tile([C, S], F32, name="kern")
         for sq, (lo, hi) in zip(sums, PARTS):
@@ -60,8 +65,10 @@ def tile_kernelgaactivation_kernel(tc, x, weight, offs, out):
         own = held.tile([C, S], F32, name="own")
         nc.vector.tensor_scalar(own[:], nodes[:], 0.0, mix[:, 0:1], op0=MAX, op1=MULT)
         result = held.tile([C, S], F32, name="result")
-        for lo, hi in PARTS:
-            nc.vector.scalar_tensor_tensor(
-                result[:, lo:hi], kern[:, lo:hi], kern_weight[:], own[:, lo:hi], op0=MULT, op1=ADD
-            )
-            nc.sync.dma_start(out[:, lo:hi], result[:, lo:hi])
+        for half_lo, half_hi in HALVES:
+            for lo, hi in PARTS:
+                if half_lo <= lo and hi <= half_hi:
+                    nc.vector.scalar_tensor_tensor(
+                        result[:, lo:hi], kern[:, lo:hi], kern_weight[:], own[:, lo:hi], op0=MULT, op1=ADD
+                    )
+            nc.sync.dma_start(out[:, half_lo:half_hi], result[:, half_lo:half_hi])

@@ -51,7 +51,10 @@ def tile_kernelgaactivation_kernel(tc, x, weight, offs, out):
             diff = held.tile([C, hi - lo], F32, name=f"diff{d}_{lo}")
             nc.vector.tensor_tensor(diff[:], nodes[:].indirect(piece), negated[:, lo:hi], ADD)
             square = held.tile([C, hi - lo], BF16, name=f"square{d}_{lo}")
-            nc.scalar.activation(square[:], diff[:], SQUARE)
+            if (d, (lo, hi)) == LOOK_UPS[-1]:
+                nc.vector.tensor_tensor(square[:], diff[:], diff[:], MULT)
+            else:
+                nc.scalar.activation(square[:], diff[:], SQUARE)
             for sq, (part_lo, part_hi) in zip(sums, PARTS):
                 if lo <= part_lo and part_hi <= hi:
                     nc.tensor.matmul(

@@ -13,8 +13,9 @@ TWO_SIGMA_SQ = 0.02
 PER_COLUMN = 16
 HALVES = [(0, 128), (128, 256)]
 PARTS = [(0, 128), (128, 192), (192, 256)]
+FIRST_CUT = 64
 LOOK_UPS = (
-    [(0, (0, S)), (1, (0, S))]
+    [(0, (0, FIRST_CUT, S)), (1, (0, S))]
     + [(2, HALVES[0]), (3, HALVES[0])]
     + [(2, HALVES[1]), (3, PARTS[1]), (3, PARTS[2])]
 )
@@ -36,7 +37,8 @@ def tile_kernelgaactivation_kernel(tc, x, weight, offs, out):
         nc.sync.dma_start(mix[:], weight.rearrange("a b -> (a b)").partition_broadcast(C))
 
         negated = held.tile([C, S], F32, name="negated")
-        nc.vector.tensor_scalar_mul(negated[:], nodes[:], -1.0)
+        for lo, hi in [(0, FIRST_CUT), (FIRST_CUT, S)]:
+            nc.vector.tensor_scalar_mul(negated[:, lo:hi], nodes[:, lo:hi], -1.0)
 
         ones = held.tile([C, C], BF16, name="ones")
         nc.gpsimd.memset(ones[:], 1.0)
@@ -46,12 +48,14 @@ def tile_kernelgaactivation_kernel(tc, x, weight, offs, out):
 
         sums = [psum.tile([C, hi - lo], F32, name=f"sq{lo}") for lo, hi in PARTS]
 
-        for d, (lo, hi) in LOOK_UPS:
-            piece = offsets[:, (d * S + lo) // PER_COLUMN : (d * S + hi) // PER_COLUMN]
+        for d, cuts in LOOK_UPS:
+            lo, hi = cuts[0], cuts[-1]
             diff = held.tile([C, hi - lo], F32, name=f"diff{d}_{lo}")
-            nc.vector.tensor_tensor(diff[:], nodes[:].indirect(piece), negated[:, lo:hi], ADD)
+            for at, end in zip(cuts, cuts[1:]):
+                piece = offsets[:, (d * S + at) // PER_COLUMN : (d * S + end) // PER_COLUMN]
+                nc.vector.tensor_tensor(diff[:, at - lo : end - lo], nodes[:].indirect(piece), negated[:, at:end], ADD)
             square = held.tile([C, hi - lo], BF16, name=f"square{d}_{lo}")
-            if (d, (lo, hi)) == LOOK_UPS[-1]:
+            if (d, cuts) == LOOK_UPS[-1]:
                 nc.vector.tensor_tensor(square[:], diff[:], diff[:], MULT)
             else:
                 nc.scalar.activation(square[:], diff[:], SQUARE)

@@ -11,13 +11,13 @@ D = 4
 N = D * S
 TWO_SIGMA_SQ = 0.02
 PER_COLUMN = 16
-HALVES = [(0, 128), (128, 256)]
+STORES = [(0, 192), (192, 256)]
 PARTS = [(0, 128), (128, 192), (192, 256)]
 FIRST_CUT = 64
 LOOK_UPS = (
     [(0, (0, FIRST_CUT, S)), (1, (0, S))]
-    + [(2, HALVES[0]), (3, HALVES[0])]
-    + [(2, HALVES[1]), (3, PARTS[1]), (3, PARTS[2])]
+    + [(2, STORES[0]), (3, PARTS[0]), (3, PARTS[1])]
+    + [(2, PARTS[2]), (3, PARTS[2])]
 )
 
 FLOPS = 3 * C * N + 4 * C * S
@@ -72,10 +72,10 @@ def tile_kernelgaactivation_kernel(tc, x, weight, offs, out):
         own = held.tile([C, S], F32, name="own")
         nc.vector.tensor_scalar(own[:], nodes[:], 0.0, mix[:, 0:1], op0=MAX, op1=MULT)
         result = held.tile([C, S], F32, name="result")
-        for half_lo, half_hi in HALVES:
+        for store_lo, store_hi in STORES:
             for lo, hi in PARTS:
-                if half_lo <= lo and hi <= half_hi:
+                if store_lo <= lo and hi <= store_hi:
                     nc.vector.scalar_tensor_tensor(
                         result[:, lo:hi], kern[:, lo:hi], kern_weight[:], own[:, lo:hi], op0=MULT, op1=ADD
                     )
-            nc.sync.dma_start(out[:, half_lo:half_hi], result[:, half_lo:half_hi])
+            nc.sync.dma_start(out[:, store_lo:store_hi], result[:, store_lo:store_hi])

@@ -11,13 +11,13 @@ D = 4
 N = D * S
 TWO_SIGMA_SQ = 0.02
 PER_COLUMN = 16
-STORES = [(0, 192), (192, 256)]
-PARTS = [(0, 128), (128, 192), (192, 256)]
+BLOCKS = [(0, 192), (192, 256)]
+PARTS = [(0, 96), (96, 192), (192, 256)]
 FIRST_CUT = 64
 LOOK_UPS = (
-    [(0, (0, FIRST_CUT, S)), (1, (0, S))]
-    + [(2, STORES[0]), (3, PARTS[0]), (3, PARTS[1])]
-    + [(2, PARTS[2]), (3, PARTS[2])]
+    [(0, (0, FIRST_CUT, S))]
+    + [(1, BLOCKS[0]), (2, BLOCKS[0]), (3, PARTS[0]), (3, PARTS[1])]
+    + [(1, BLOCKS[1]), (2, BLOCKS[1]), (3, BLOCKS[1])]
 )
 
 FLOPS = 3 * C * N + 4 * C * S
@@ -72,10 +72,10 @@ def tile_kernelgaactivation_kernel(tc, x, weight, offs, out):
         own = held.tile([C, S], F32, name="own")
         nc.vector.tensor_scalar(own[:], nodes[:], 0.0, mix[:, 0:1], op0=MAX, op1=MULT)
         result = held.tile([C, S], F32, name="result")
-        for store_lo, store_hi in STORES:
+        for block_lo, block_hi in BLOCKS:
             for lo, hi in PARTS:
-                if store_lo <= lo and hi <= store_hi:
+                if block_lo <= lo and hi <= block_hi:
                     nc.vector.scalar_tensor_tensor(
                         result[:, lo:hi], kern[:, lo:hi], kern_weight[:], own[:, lo:hi], op0=MULT, op1=ADD
                     )
-            nc.sync.dma_start(out[:, store_lo:store_hi], result[:, store_lo:store_hi])
+            nc.sync.dma_start(out[:, block_lo:block_hi], result[:, block_lo:block_hi])

@@ -36,12 +36,12 @@ def tile_kernelgaactivation_kernel(tc, x, weight, offs, out):
         mix = held.tile([C, 3], F32, name="mix")
         nc.sync.dma_start(mix[:], weight.rearrange("a b -> (a b)").partition_broadcast(C))
 
+        ones = held.tile([C, C], BF16, name="ones")
+        nc.vector.memset(ones[:], 1.0)
+
         negated = held.tile([C, S], F32, name="negated")
         for lo, hi in [(0, FIRST_CUT), (FIRST_CUT, S)]:
             nc.vector.tensor_scalar_mul(negated[:, lo:hi], nodes[:, lo:hi], -1.0)
-
-        ones = held.tile([C, C], BF16, name="ones")
-        nc.gpsimd.memset(ones[:], 1.0)
 
         kern_weight = held.tile([C, 1], F32, name="kern_weight")
         nc.scalar.activation(kern_weight[:], mix[:, 1:2], IDENTITY, bias=mix[:, 2:3])

import concourse.mybir as mybir

F32, BF16, U16 = mybir.dt.float32, mybir.dt.bfloat16, mybir.dt.uint16
ADD, MULT, MAX = mybir.AluOpType.add, mybir.AluOpType.mult, mybir.AluOpType.max
SQUARE, EXP = mybir.ActivationFunctionType.Square, mybir.ActivationFunctionType.Exp
IDENTITY = mybir.ActivationFunctionType.Identity

C = 128
S = 256
D = 4
N = D * S
TWO_SIGMA_SQ = 0.02
PER_COLUMN = 16
BLOCKS = [(0, 192), (192, 256)]
PARTS = [(0, 96), (96, 192), (192, 256)]
FIRST_CUT = 64
LOOK_UPS = (
    [(0, (0, FIRST_CUT, S))]
    + [(1, BLOCKS[0]), (2, BLOCKS[0]), (3, PARTS[0]), (3, PARTS[1])]
    + [(1, BLOCKS[1]), (2, BLOCKS[1]), (3, BLOCKS[1])]
)

FLOPS = 3 * C * N + 4 * C * S


def tile_kernelgaactivation_kernel(tc, x, weight, offs, out):
    nc = tc.nc
    with (
        tc.tile_pool(name="held", bufs=1) as held,
        tc.psum_pool(name="psum", bufs=1) as psum,
    ):
        offsets = held.tile([C, N // PER_COLUMN], U16, name="offsets")
        nc.sync.dma_start(offsets[:], offs)
        nodes = held.tile([C, S], F32, name="nodes")
        nc.scalar.dma_start(nodes[:], x)
        mix = held.tile([C, 3], F32, name="mix")
        nc.sync.dma_start(mix[:], weight.rearrange("a b -> (a b)").partition_broadcast(C))

        ones = held.tile([C, C], BF16, name="ones")
        nc.vector.memset(ones[:], 1.0)

        negated = held.tile([C, S], F32, name="negated")
        for lo, hi in [(0, FIRST_CUT), (FIRST_CUT, S)]:
            nc.vector.tensor_scalar_mul(negated[:, lo:hi], nodes[:, lo:hi], -1.0)

        kern_weight = held.tile([C, 1], F32, name="kern_weight")
        nc.scalar.activation(kern_weight[:], mix[:, 1:2], IDENTITY, bias=mix[:, 2:3])

        sums = [psum.tile([C, hi - lo], F32, name=f"sq{lo}") for lo, hi in PARTS]

        for d, cuts in LOOK_UPS:
            lo, hi = cuts[0], cuts[-1]
            diff = held.tile([C, hi - lo], F32, name=f"diff{d}_{lo}")
            for at, end in zip(cuts, cuts[1:]):
                piece = offsets[:, (d * S + at) // PER_COLUMN : (d * S + end) // PER_COLUMN]
                nc.vector.tensor_tensor(diff[:, at - lo : end - lo], nodes[:].indirect(piece), negated[:, at:end], ADD)
            square = held.tile([C, hi - lo], BF16, name=f"square{d}_{lo}")
            if (d, cuts) == LOOK_UPS[-1]:
                nc.vector.tensor_tensor(square[:], diff[:], diff[:], MULT)
            else:
                nc.scalar.activation(square[:], diff[:], SQUARE)
            for sq, (part_lo, part_hi) in zip(sums, PARTS):
                if lo <= part_lo and part_hi <= hi:
                    nc.tensor.matmul(
                        sq[:], ones[:], square[:, part_lo - lo : part_hi - lo], start=(d == 0), stop=(d == D - 1)
                    )

        kern = held.tile([C, S], F32, name="kern")
        for sq, (lo, hi) in zip(sums, PARTS):
            nc.scalar.activation(kern[:, lo:hi], sq[:], EXP, scale=-1.0 / TWO_SIGMA_SQ)

        own = held.tile([C, S], F32, name="own")
        nc.vector.tensor_scalar(own[:], nodes[:], 0.0, mix[:, 0:1], op0=MAX, op1=MULT)
        result = held.tile([C, S], F32, name="result")
        for block_lo, block_hi in BLOCKS:
            for lo, hi in PARTS:
                if block_lo <= lo and hi <= block_hi:
                    nc.vector.scalar_tensor_tensor(
                        result[:, lo:hi], kern[:, lo:hi], kern_weight[:], own[:, lo:hi], op0=MULT, op1=ADD
                    )
            nc.sync.dma_start(out[:, block_lo:block_hi], result[:, block_lo:block_hi])
